import numpy as np
import ml_dtypes


def mxq(x, axis, fmt="e4m3"):
    dtype, down = {"e4m3": (ml_dtypes.float8_e4m3fn, 7), "e5m2": (ml_dtypes.float8_e5m2, 14)}[fmt]
    v = np.moveaxis(np.asarray(x, np.float32).astype(ml_dtypes.bfloat16).astype(np.float64), axis, -1)
    blocks = v.reshape(v.shape[:-1] + (-1, 32))
    amax = np.abs(blocks).max(-1, keepdims=True)
    byte = np.maximum(np.where(amax > 0, np.frexp(amax)[1] - 1 + 127, 0) - down, 1)
    scale = np.exp2(byte - 127.0)
    codes = (blocks / scale).astype(np.float32).astype(dtype).astype(np.float64)
    return np.moveaxis((codes * scale).reshape(v.shape), -1, axis)


WIDE = False


def mx_kscale(k):
    if not WIDE:
        return np.ones(k)
    levels = np.array([10, -10, 5, -5, 0])
    a = np.random.permutation(np.resize(levels, k // 512 * 4)).reshape(k // 512, 4)
    idx = np.arange(k)
    return np.exp2(a[idx // 512, idx % 128 // 32])


BF16 = ml_dtypes.bfloat16


def bf(x):
    return np.asarray(x, np.float32).astype(BF16)


def f64(x):
    return np.asarray(x).astype(np.float64)


E2M1 = np.array([0.0, 0.5, 1.0, 1.5, 2.0, 3.0, 4.0, 6.0, -0.0, -0.5, -1.0, -1.5, -2.0, -3.0, -4.0, -6.0])


def pack_weight(w, fmt):
    k, n = w.shape
    w = f64(bf(w)).reshape(k // 32, 32, n)
    amax = np.abs(w).max(1)
    if fmt == "e4m3":
        byte = np.frexp(amax)[1] - 1 + 127 - 7
    else:
        mant, ex = np.frexp(amax / 6.0)
        byte = np.where(mant > 0.5, ex, ex - 1) + 127
    byte = np.clip(np.where(amax > 0, byte, 1), 1, 254)
    scaled = (w * np.exp2(127.0 - byte)[:, None, :]).reshape(k, n).astype(np.float32)
    by_word = np.ascontiguousarray(scaled.reshape(k // 512, 128, 4, n).transpose(0, 1, 3, 2))
    if fmt == "e4m3":
        words = by_word.astype(ml_dtypes.float8_e4m3fn).view(np.uint8)
    else:
        c = by_word.astype(ml_dtypes.float4_e2m1fn).view(np.uint8) & 0xF
        words = c[..., 0::2] | (c[..., 1::2] << 4)
    return np.ascontiguousarray(words), np.ascontiguousarray(byte.astype(np.uint8).reshape(k // 512, 16, n))


def unpack_weight(words, scales, fmt):
    g, p, n, _ = words.shape
    if fmt == "e4m3":
        vals = np.ascontiguousarray(words).view(ml_dtypes.float8_e4m3fn).astype(np.float64)
    else:
        nib = np.empty((g, p, n, 4), np.uint8)
        nib[..., 0::2] = words & 0xF
        nib[..., 1::2] = words >> 4
        vals = E2M1[nib]
    vals = vals * np.repeat(np.exp2(scales.astype(np.float64) - 127.0), 8, axis=1)[..., None]
    return vals.transpose(0, 1, 3, 2).reshape(g * 512, n)


N, E, C = 2048, 1024, 512
DENSITY = 0.01
HE_RMS = np.sqrt(np.e / E)


def setup_inputs():
    s, t = mx_kscale(E), mx_kscale(C)
    member = np.random.uniform(size=(N, E)) < DENSITY
    incidence = bf(member * s[None, :])
    he = bf(np.random.standard_normal((E, C)) * HE_RMS / s[:, None] * t[None, :])
    W2_words, W2_scales = pack_weight(np.random.standard_normal((C, C)) * 3.0 / np.sqrt(C) / t[:, None], "e4m3")
    return {"incidence": incidence,
            "he": he,
            "W2_words": W2_words,
            "W2_scales": W2_scales,
            "b2": bf(np.random.standard_normal(C) * 0.2),
            "node_features": bf(np.random.standard_normal((N, C)))}


def reference(incidence, he, W2_words, W2_scales, b2, node_features):
    prop = mxq(f64(incidence), 1, "e4m3") @ mxq(f64(he), 0, "e4m3")
    return (mxq(prop, 1, "e4m3") @ unpack_weight(W2_words, W2_scales, "e4m3")) + f64(b2) + f64(node_features)

@@ -1,0 +1,201 @@
+from contextlib import ExitStack
+
+import concourse.mybir as mybir
+from concourse.masks import make_identity
+
+BF16 = mybir.dt.bfloat16
+F32 = mybir.dt.float32
+I32 = mybir.dt.int32
+U32 = mybir.dt.uint32
+U8 = mybir.dt.uint8
+FP8X4 = mybir.dt.float8_e4m3fn_x4
+ADD = mybir.AluOpType.add
+
+P = 128
+PACK = 4
+K_PASS = P * PACK
+
+NODES, EDGES, CHANNELS = 2048, 1024, 512
+EDGE_PASSES = EDGES // K_PASS
+BLOCK = P
+CHUNK_BLOCKS = 4
+UNIT_BLOCKS = 2
+CHUNKS = NODES // (CHUNK_BLOCKS * BLOCK)
+UNITS = NODES // (UNIT_BLOCKS * BLOCK)
+UNITS_PER_CHUNK = CHUNK_BLOCKS // UNIT_BLOCKS
+
+FLOPS = 2 * NODES * EDGES * CHANNELS + 2 * NODES * CHANNELS * CHANNELS
+
+
+def tile_heterogeneoustemporalhypergraphnn_pb_kernel(
+    tc, incidence, he, W2_words, W2_scales, b2, node_features, out
+):
+    nc = tc.nc
+    with ExitStack() as ctx:
+        ctx.enter_context(tc.manual_schedule())
+        keep = ctx.enter_context(tc.tile_pool(name="keep", bufs=1))
+        inc_pool = ctx.enter_context(tc.tile_pool(name="inc", bufs=UNITS))
+        nf_pool = ctx.enter_context(tc.tile_pool(name="nf", bufs=CHUNKS))
+        work = ctx.enter_context(tc.tile_pool(name="work", bufs=3))
+        late = ctx.enter_context(tc.tile_pool(name="late", bufs=4))
+        psum_t = ctx.enter_context(tc.psum_pool(name="psum_t", bufs=2))
+        psum_p = ctx.enter_context(tc.psum_pool(name="psum_p", bufs=2))
+        psum_o = ctx.enter_context(tc.psum_pool(name="psum_o", bufs=4))
+
+        inc_v = incidence.rearrange("(c p j) e -> c p j e", p=P, j=CHUNK_BLOCKS)
+        nf_v = node_features.rearrange("(c p j) n -> c p j n", p=P, j=CHUNK_BLOCKS)
+        out_v = out.rearrange("(c p j) n -> c p j n", p=P, j=CHUNK_BLOCKS)
+        he_v = he.rearrange("(g u p e) n -> g p u e n", g=EDGE_PASSES, u=2, p=P, e=2)
+
+        ident = keep.tile([P, P], F32)
+        make_identity(nc, ident[:])
+        ones = keep.tile([P, P], BF16)
+        nc.vector.memset(ones[:], 1.0)
+        bias_row = keep.tile([P, CHANNELS], BF16)
+        nc.vector.memset(bias_row[:], 0.0)
+        w2_plane = keep.tile([P, CHANNELS], U8, align_bytes=64)
+        nc.vector.memset(w2_plane[:].bitcast(I32), 0)
+
+        he_raw = keep.tile([P, EDGE_PASSES, PACK, CHANNELS], BF16)
+        for g in range(EDGE_PASSES):
+            nc.sync.dma_start(
+                out=he_raw[:, g].rearrange("p (u e) n -> p u e n", u=2), in_=he_v[g]
+            )
+        nc.sync.dma_start(out=bias_row[0:1, :], in_=b2.rearrange("(o n) -> o n", o=1))
+        w2_codes = keep.tile([P, CHANNELS], U32, align_bytes=64)
+        inc_of = {}
+        nf_of = {}
+        for c in range(CHUNKS):
+            for h in range(UNITS_PER_CHUNK):
+                inc_sb = inc_pool.tile([P, UNIT_BLOCKS, EDGES], BF16)
+                rows = slice(h * UNIT_BLOCKS, (h + 1) * UNIT_BLOCKS)
+                nc.sync.dma_start(out=inc_sb[:], in_=inc_v[c][:, rows, :])
+                inc_of[c * UNITS_PER_CHUNK + h] = inc_sb
+            if c == 0:
+                nc.sync.dma_start(
+                    out=w2_codes[:].bitcast(I32),
+                    in_=W2_words[0].rearrange("p n t -> p (n t)").bitcast(I32),
+                )
+                for quad in range(4):
+                    nc.sync.dma_start(
+                        out=w2_plane[32 * quad : 32 * quad + 4, :].bitcast(I32),
+                        in_=W2_scales[0][4 * quad : 4 * quad + 4, :].bitcast(I32),
+                    )
+            nf_sb = nf_pool.tile([P, CHUNK_BLOCKS, CHANNELS], BF16)
+            nc.sync.dma_start(out=nf_sb[:], in_=nf_v[c])
+            nf_of[c] = nf_sb
+
+        bias_ps = psum_o.tile([P, CHANNELS], F32, tag="second")
+        nc.tensor.matmul(out=bias_ps[:], lhsT=ones[:], rhs=bias_row[:], start=True, stop=True)
+        bias_all = keep.tile([P, CHANNELS], F32)
+        nc.scalar.copy(out=bias_all[:], in_=bias_ps[:])
+
+        he_grouped = keep.tile([P, EDGE_PASSES, PACK, P, PACK], BF16, align_bytes=64)
+        he_codes = keep.tile([P, EDGE_PASSES, CHANNELS], U32, align_bytes=64)
+        he_scales = keep.tile([P, EDGE_PASSES, CHANNELS], U8, align_bytes=64)
+        for g in range(EDGE_PASSES):
+            nc.vector.tensor_copy(
+                out=he_grouped[:, g],
+                in_=he_raw[:, g].rearrange("p t (m q) -> p q m t", q=PACK),
+            )
+        for g in range(EDGE_PASSES):
+            nc.vector.quantize_mx(
+                out=he_codes[:, g, :].bitcast(FP8X4),
+                scales=he_scales[:, g, :],
+                in_=he_grouped[:, g].rearrange("p q m t -> p (q m t)"),
+            )
+
+        inc_q = {}
+        prop_q = {}
+        base_of = {}
+
+        def transpose_and_quantise(u):
+            grouped = work.tile([P, UNIT_BLOCKS, EDGE_PASSES, BLOCK, PACK], BF16, align_bytes=64)
+            for a in range(UNIT_BLOCKS):
+                words = inc_of[u][:, a, :].bitcast(F32)
+                flipped = psum_t.tile([P, EDGE_PASSES * 2, BLOCK], F32)
+                for w in range(EDGE_PASSES * 2):
+                    nc.tensor.transpose(flipped[:, w, :], words[:, w * P : (w + 1) * P], ident[:])
+                nc.scalar.copy(
+                    out=grouped[:, a].bitcast(F32),
+                    in_=flipped[:].rearrange("p (g u) n -> p g n u", u=2),
+                )
+            codes = work.tile([P, UNIT_BLOCKS, EDGE_PASSES, BLOCK], U32, align_bytes=64)
+            scales = work.tile([P, UNIT_BLOCKS, EDGE_PASSES, BLOCK], U8, align_bytes=64)
+            nc.vector.quantize_mx(
+                out=codes[:].rearrange("p a g n -> p (a g n)").bitcast(FP8X4),
+                scales=scales[:].rearrange("p a g n -> p (a g n)"),
+                in_=grouped[:].rearrange("p a g n t -> p (a g n t)"),
+            )
+            inc_q[u] = (codes, scales)
+
+        def add_bias_to_residual(u):
+            base = late.tile([P, UNIT_BLOCKS, CHANNELS], F32)
+            first = (u % UNITS_PER_CHUNK) * UNIT_BLOCKS
+            nc.vector.tensor_tensor(
+                out=base[:],
+                in0=nf_of[u // UNITS_PER_CHUNK][:, first : first + UNIT_BLOCKS, :],
+                in1=bias_all[:].unsqueeze(1).to_broadcast([P, UNIT_BLOCKS, CHANNELS]),
+                op=ADD,
+            )
+            base_of[u] = base
+
+        def first_product(u):
+            codes, scales = inc_q[u]
+            prop_grouped = work.tile([P, UNIT_BLOCKS, BLOCK, PACK], BF16, align_bytes=64)
+            for a in range(UNIT_BLOCKS):
+                prop_ps = psum_p.tile([P, PACK, BLOCK], F32)
+                for q in range(PACK):
+                    cols = slice(q * P, (q + 1) * P)
+                    for g in range(EDGE_PASSES):
+                        nc.tensor.matmul_mx(
+                            out=prop_ps[:, q, :],
+                            lhsT=he_codes[:, g, cols].bitcast(FP8X4),
+                            lhsT_scale=he_scales[:, g, cols],
+                            rhs=codes[:, a, g, :].bitcast(FP8X4),
+                            rhs_scale=scales[:, a, g, :],
+                            start=(g == 0),
+                            stop=(g == EDGE_PASSES - 1),
+                        )
+                nc.scalar.copy(
+                    out=prop_grouped[:, a], in_=prop_ps[:].rearrange("p q n -> p n q")
+                )
+            prop_codes = work.tile([P, UNIT_BLOCKS, BLOCK], U32, align_bytes=64)
+            prop_scales = work.tile([P, UNIT_BLOCKS, BLOCK], U8, align_bytes=64)
+            nc.vector.quantize_mx(
+                out=prop_codes[:].rearrange("p a n -> p (a n)").bitcast(FP8X4),
+                scales=prop_scales[:].rearrange("p a n -> p (a n)"),
+                in_=prop_grouped[:].rearrange("p a n t -> p (a n t)"),
+            )
+            prop_q[u] = (prop_codes, prop_scales)
+
+        def second_product(u):
+            prop_codes, prop_scales = prop_q[u]
+            result = late.tile([P, UNIT_BLOCKS, CHANNELS], F32)
+            for a in range(UNIT_BLOCKS):
+                second = psum_o.tile([P, CHANNELS], F32)
+                nc.tensor.matmul_mx(
+                    out=second[:],
+                    lhsT=prop_codes[:, a, :].bitcast(FP8X4),
+                    lhsT_scale=prop_scales[:, a, :],
+                    rhs=w2_codes[:].bitcast(FP8X4),
+                    rhs_scale=w2_plane[:],
+                    start=True,
+                    stop=True,
+                )
+                nc.vector.tensor_tensor(
+                    out=result[:, a, :], in0=second[:], in1=base_of[u][:, a, :], op=ADD
+                )
+            first = (u % UNITS_PER_CHUNK) * UNIT_BLOCKS
+            nc.sync.dma_start(
+                out=out_v[u // UNITS_PER_CHUNK][:, first : first + UNIT_BLOCKS, :], in_=result[:]
+            )
+
+        for k in range(UNITS + 2):
+            if k < UNITS:
+                transpose_and_quantise(k)
+                add_bias_to_residual(k)
+            if 1 <= k <= UNITS:
+                first_product(k - 1)
+            if k >= 2:
+                second_product(k - 2)

@@ -132,12 +132,14 @@ def tile_heterogeneoustemporalhypergraphnn_pb_kernel(
         def add_bias_to_residual(u):
             base = late.tile([P, UNIT_BLOCKS, CHANNELS], F32)
             first = (u % UNITS_PER_CHUNK) * UNIT_BLOCKS
-            nc.vector.tensor_tensor(
-                out=base[:],
-                in0=nf_of[u // UNITS_PER_CHUNK][:, first : first + UNIT_BLOCKS, :],
-                in1=bias_all[:].unsqueeze(1).to_broadcast([P, UNIT_BLOCKS, CHANNELS]),
-                op=ADD,
-            )
+            adder = nc.vector if u % 2 == 0 else nc.gpsimd
+            for a in range(UNIT_BLOCKS):
+                adder.tensor_tensor(
+                    out=base[:, a, :],
+                    in0=nf_of[u // UNITS_PER_CHUNK][:, first + a, :],
+                    in1=bias_all[:],
+                    op=ADD,
+                )
             base_of[u] = base
 
         def first_product(u):

@@ -57,20 +57,32 @@ def tile_heterogeneoustemporalhypergraphnn_pb_kernel(
         nc.vector.memset(w2_plane[:].bitcast(I32), 0)
 
         he_raw = keep.tile([P, EDGE_PASSES, PACK, CHANNELS], BF16)
-        for g in range(EDGE_PASSES):
-            nc.sync.dma_start(
-                out=he_raw[:, g].rearrange("p (u e) n -> p u e n", u=2), in_=he_v[g]
-            )
-        nc.sync.dma_start(out=bias_row[0:1, :], in_=b2.rearrange("(o n) -> o n", o=1))
         w2_codes = keep.tile([P, CHANNELS], U32, align_bytes=64)
         inc_of = {}
         nf_of = {}
+
+        def load_he(g):
+            nc.sync.dma_start(
+                out=he_raw[:, g].rearrange("p (u e) n -> p u e n", u=2), in_=he_v[g]
+            )
+
+        def load_incidence(u):
+            inc_sb = inc_pool.tile([P, UNIT_BLOCKS, EDGES], BF16)
+            first = (u % UNITS_PER_CHUNK) * UNIT_BLOCKS
+            nc.sync.dma_start(
+                out=inc_sb[:], in_=inc_v[u // UNITS_PER_CHUNK][:, first : first + UNIT_BLOCKS, :]
+            )
+            inc_of[u] = inc_sb
+
+        load_he(0)
+        load_incidence(0)
+        load_he(1)
+        nc.sync.dma_start(out=bias_row[0:1, :], in_=b2.rearrange("(o n) -> o n", o=1))
+        load_incidence(1)
         for c in range(CHUNKS):
-            for h in range(UNITS_PER_CHUNK):
-                inc_sb = inc_pool.tile([P, UNIT_BLOCKS, EDGES], BF16)
-                rows = slice(h * UNIT_BLOCKS, (h + 1) * UNIT_BLOCKS)
-                nc.sync.dma_start(out=inc_sb[:], in_=inc_v[c][:, rows, :])
-                inc_of[c * UNITS_PER_CHUNK + h] = inc_sb
+            if c > 0:
+                for h in range(UNITS_PER_CHUNK):
+                    load_incidence(c * UNITS_PER_CHUNK + h)
             if c == 0:
                 nc.sync.dma_start(
                     out=w2_codes[:].bitcast(I32),
@@ -85,10 +97,12 @@ def tile_heterogeneoustemporalhypergraphnn_pb_kernel(
             nc.sync.dma_start(out=nf_sb[:], in_=nf_v[c])
             nf_of[c] = nf_sb
 
-        bias_ps = psum_o.tile([P, CHANNELS], F32, tag="second")
-        nc.tensor.matmul(out=bias_ps[:], lhsT=ones[:], rhs=bias_row[:], start=True, stop=True)
         bias_all = keep.tile([P, CHANNELS], F32)
-        nc.scalar.copy(out=bias_all[:], in_=bias_ps[:])
+
+        def broadcast_bias():
+            bias_ps = psum_o.tile([P, CHANNELS], F32, tag="second")
+            nc.tensor.matmul(out=bias_ps[:], lhsT=ones[:], rhs=bias_row[:], start=True, stop=True)
+            nc.scalar.copy(out=bias_all[:], in_=bias_ps[:])
 
         he_grouped = keep.tile([P, EDGE_PASSES, PACK, P, PACK], BF16, align_bytes=64)
         he_codes = keep.tile([P, EDGE_PASSES, CHANNELS], U32, align_bytes=64)
@@ -98,7 +112,6 @@ def tile_heterogeneoustemporalhypergraphnn_pb_kernel(
                 out=he_grouped[:, g],
                 in_=he_raw[:, g].rearrange("p t (m q) -> p q m t", q=PACK),
             )
-        for g in range(EDGE_PASSES):
             nc.vector.quantize_mx(
                 out=he_codes[:, g, :].bitcast(FP8X4),
                 scales=he_scales[:, g, :],
@@ -132,14 +145,12 @@ def tile_heterogeneoustemporalhypergraphnn_pb_kernel(
         def add_bias_to_residual(u):
             base = late.tile([P, UNIT_BLOCKS, CHANNELS], F32)
             first = (u % UNITS_PER_CHUNK) * UNIT_BLOCKS
-            adder = nc.vector if u % 2 == 0 else nc.gpsimd
-            for a in range(UNIT_BLOCKS):
-                adder.tensor_tensor(
-                    out=base[:, a, :],
-                    in0=nf_of[u // UNITS_PER_CHUNK][:, first + a, :],
-                    in1=bias_all[:],
-                    op=ADD,
-                )
+            nc.vector.tensor_tensor(
+                out=base[:],
+                in0=nf_of[u // UNITS_PER_CHUNK][:, first : first + UNIT_BLOCKS, :],
+                in1=bias_all[:].unsqueeze(1).to_broadcast([P, UNIT_BLOCKS, CHANNELS]),
+                op=ADD,
+            )
             base_of[u] = base
 
         def first_product(u):
@@ -188,14 +199,14 @@ def tile_heterogeneoustemporalhypergraphnn_pb_kernel(
                 nc.vector.tensor_tensor(
                     out=result[:, a, :], in0=second[:], in1=base_of[u][:, a, :], op=ADD
                 )
-            first = (u % UNITS_PER_CHUNK) * UNIT_BLOCKS
-            nc.sync.dma_start(
-                out=out_v[u // UNITS_PER_CHUNK][:, first : first + UNIT_BLOCKS, :], in_=result[:]
-            )
+                j = (u % UNITS_PER_CHUNK) * UNIT_BLOCKS + a
+                nc.sync.dma_start(out=out_v[u // UNITS_PER_CHUNK][:, j, :], in_=result[:, a, :])
 
         for k in range(UNITS + 2):
             if k < UNITS:
                 transpose_and_quantise(k)
+                if k == 0:
+                    broadcast_bias()
                 add_bias_to_residual(k)
             if 1 <= k <= UNITS:
                 first_product(k - 1)

from contextlib import ExitStack

import concourse.mybir as mybir
from concourse.masks import make_identity

BF16 = mybir.dt.bfloat16
F32 = mybir.dt.float32
I32 = mybir.dt.int32
U32 = mybir.dt.uint32
U8 = mybir.dt.uint8
FP8X4 = mybir.dt.float8_e4m3fn_x4
ADD = mybir.AluOpType.add

P = 128
PACK = 4
K_PASS = P * PACK

NODES, EDGES, CHANNELS = 2048, 1024, 512
EDGE_PASSES = EDGES // K_PASS
BLOCK = P
CHUNK_BLOCKS = 4
UNIT_BLOCKS = 2
CHUNKS = NODES // (CHUNK_BLOCKS * BLOCK)
UNITS = NODES // (UNIT_BLOCKS * BLOCK)
UNITS_PER_CHUNK = CHUNK_BLOCKS // UNIT_BLOCKS

FLOPS = 2 * NODES * EDGES * CHANNELS + 2 * NODES * CHANNELS * CHANNELS


def tile_heterogeneoustemporalhypergraphnn_pb_kernel(
    tc, incidence, he, W2_words, W2_scales, b2, node_features, out
):
    nc = tc.nc
    with ExitStack() as ctx:
        ctx.enter_context(tc.manual_schedule())
        keep = ctx.enter_context(tc.tile_pool(name="keep", bufs=1))
        inc_pool = ctx.enter_context(tc.tile_pool(name="inc", bufs=UNITS))
        nf_pool = ctx.enter_context(tc.tile_pool(name="nf", bufs=CHUNKS))
        work = ctx.enter_context(tc.tile_pool(name="work", bufs=3))
        late = ctx.enter_context(tc.tile_pool(name="late", bufs=4))
        psum_t = ctx.enter_context(tc.psum_pool(name="psum_t", bufs=2))
        psum_p = ctx.enter_context(tc.psum_pool(name="psum_p", bufs=2))
        psum_o = ctx.enter_context(tc.psum_pool(name="psum_o", bufs=4))

        inc_v = incidence.rearrange("(c p j) e -> c p j e", p=P, j=CHUNK_BLOCKS)
        nf_v = node_features.rearrange("(c p j) n -> c p j n", p=P, j=CHUNK_BLOCKS)
        out_v = out.rearrange("(c p j) n -> c p j n", p=P, j=CHUNK_BLOCKS)
        he_v = he.rearrange("(g u p e) n -> g p u e n", g=EDGE_PASSES, u=2, p=P, e=2)

        ident = keep.tile([P, P], F32)
        make_identity(nc, ident[:])
        ones = keep.tile([P, P], BF16)
        nc.vector.memset(ones[:], 1.0)
        bias_row = keep.tile([P, CHANNELS], BF16)
        nc.vector.memset(bias_row[:], 0.0)
        w2_plane = keep.tile([P, CHANNELS], U8, align_bytes=64)
        nc.vector.memset(w2_plane[:].bitcast(I32), 0)

        he_raw = keep.tile([P, EDGE_PASSES, PACK, CHANNELS], BF16)
        w2_codes = keep.tile([P, CHANNELS], U32, align_bytes=64)
        inc_of = {}
        nf_of = {}

        def load_he(g):
            nc.sync.dma_start(
                out=he_raw[:, g].rearrange("p (u e) n -> p u e n", u=2), in_=he_v[g]
            )

        def load_incidence(u):
            inc_sb = inc_pool.tile([P, UNIT_BLOCKS, EDGES], BF16)
            first = (u % UNITS_PER_CHUNK) * UNIT_BLOCKS
            nc.sync.dma_start(
                out=inc_sb[:], in_=inc_v[u // UNITS_PER_CHUNK][:, first : first + UNIT_BLOCKS, :]
            )
            inc_of[u] = inc_sb

        load_he(0)
        load_incidence(0)
        load_he(1)
        nc.sync.dma_start(out=bias_row[0:1, :], in_=b2.rearrange("(o n) -> o n", o=1))
        load_incidence(1)
        for c in range(CHUNKS):
            if c > 0:
                for h in range(UNITS_PER_CHUNK):
                    load_incidence(c * UNITS_PER_CHUNK + h)
            if c == 0:
                nc.sync.dma_start(
                    out=w2_codes[:].bitcast(I32),
                    in_=W2_words[0].rearrange("p n t -> p (n t)").bitcast(I32),
                )
                for quad in range(4):
                    nc.sync.dma_start(
                        out=w2_plane[32 * quad : 32 * quad + 4, :].bitcast(I32),
                        in_=W2_scales[0][4 * quad : 4 * quad + 4, :].bitcast(I32),
                    )
            nf_sb = nf_pool.tile([P, CHUNK_BLOCKS, CHANNELS], BF16)
            nc.sync.dma_start(out=nf_sb[:], in_=nf_v[c])
            nf_of[c] = nf_sb

        bias_all = keep.tile([P, CHANNELS], F32)

        def broadcast_bias():
            bias_ps = psum_o.tile([P, CHANNELS], F32, tag="second")
            nc.tensor.matmul(out=bias_ps[:], lhsT=ones[:], rhs=bias_row[:], start=True, stop=True)
            nc.scalar.copy(out=bias_all[:], in_=bias_ps[:])

        he_grouped = keep.tile([P, EDGE_PASSES, PACK, P, PACK], BF16, align_bytes=64)
        he_codes = keep.tile([P, EDGE_PASSES, CHANNELS], U32, align_bytes=64)
        he_scales = keep.tile([P, EDGE_PASSES, CHANNELS], U8, align_bytes=64)
        for g in range(EDGE_PASSES):
            nc.vector.tensor_copy(
                out=he_grouped[:, g],
                in_=he_raw[:, g].rearrange("p t (m q) -> p q m t", q=PACK),
            )
            nc.vector.quantize_mx(
                out=he_codes[:, g, :].bitcast(FP8X4),
                scales=he_scales[:, g, :],
                in_=he_grouped[:, g].rearrange("p q m t -> p (q m t)"),
            )

        inc_q = {}
        prop_q = {}
        base_of = {}

        def transpose_and_quantise(u):
            grouped = work.tile([P, UNIT_BLOCKS, EDGE_PASSES, BLOCK, PACK], BF16, align_bytes=64)
            for a in range(UNIT_BLOCKS):
                words = inc_of[u][:, a, :].bitcast(F32)
                flipped = psum_t.tile([P, EDGE_PASSES * 2, BLOCK], F32)
                for w in range(EDGE_PASSES * 2):
                    nc.tensor.transpose(flipped[:, w, :], words[:, w * P : (w + 1) * P], ident[:])
                nc.scalar.copy(
                    out=grouped[:, a].bitcast(F32),
                    in_=flipped[:].rearrange("p (g u) n -> p g n u", u=2),
                )
            codes = work.tile([P, UNIT_BLOCKS, EDGE_PASSES, BLOCK], U32, align_bytes=64)
            scales = work.tile([P, UNIT_BLOCKS, EDGE_PASSES, BLOCK], U8, align_bytes=64)
            nc.vector.quantize_mx(
                out=codes[:].rearrange("p a g n -> p (a g n)").bitcast(FP8X4),
                scales=scales[:].rearrange("p a g n -> p (a g n)"),
                in_=grouped[:].rearrange("p a g n t -> p (a g n t)"),
            )
            inc_q[u] = (codes, scales)

        def add_bias_to_residual(u):
            base = late.tile([P, UNIT_BLOCKS, CHANNELS], F32)
            first = (u % UNITS_PER_CHUNK) * UNIT_BLOCKS
            nc.vector.tensor_tensor(
                out=base[:],
                in0=nf_of[u // UNITS_PER_CHUNK][:, first : first + UNIT_BLOCKS, :],
                in1=bias_all[:].unsqueeze(1).to_broadcast([P, UNIT_BLOCKS, CHANNELS]),
                op=ADD,
            )
            base_of[u] = base

        def first_product(u):
            codes, scales = inc_q[u]
            prop_grouped = work.tile([P, UNIT_BLOCKS, BLOCK, PACK], BF16, align_bytes=64)
            for a in range(UNIT_BLOCKS):
                prop_ps = psum_p.tile([P, PACK, BLOCK], F32)
                for q in range(PACK):
                    cols = slice(q * P, (q + 1) * P)
                    for g in range(EDGE_PASSES):
                        nc.tensor.matmul_mx(
                            out=prop_ps[:, q, :],
                            lhsT=he_codes[:, g, cols].bitcast(FP8X4),
                            lhsT_scale=he_scales[:, g, cols],
                            rhs=codes[:, a, g, :].bitcast(FP8X4),
                            rhs_scale=scales[:, a, g, :],
                            start=(g == 0),
                            stop=(g == EDGE_PASSES - 1),
                        )
                nc.scalar.copy(
                    out=prop_grouped[:, a], in_=prop_ps[:].rearrange("p q n -> p n q")
                )
            prop_codes = work.tile([P, UNIT_BLOCKS, BLOCK], U32, align_bytes=64)
            prop_scales = work.tile([P, UNIT_BLOCKS, BLOCK], U8, align_bytes=64)
            nc.vector.quantize_mx(
                out=prop_codes[:].rearrange("p a n -> p (a n)").bitcast(FP8X4),
                scales=prop_scales[:].rearrange("p a n -> p (a n)"),
                in_=prop_grouped[:].rearrange("p a n t -> p (a n t)"),
            )
            prop_q[u] = (prop_codes, prop_scales)

        def second_product(u):
            prop_codes, prop_scales = prop_q[u]
            result = late.tile([P, UNIT_BLOCKS, CHANNELS], F32)
            for a in range(UNIT_BLOCKS):
                second = psum_o.tile([P, CHANNELS], F32)
                nc.tensor.matmul_mx(
                    out=second[:],
                    lhsT=prop_codes[:, a, :].bitcast(FP8X4),
                    lhsT_scale=prop_scales[:, a, :],
                    rhs=w2_codes[:].bitcast(FP8X4),
                    rhs_scale=w2_plane[:],
                    start=True,
                    stop=True,
                )
                nc.vector.tensor_tensor(
                    out=result[:, a, :], in0=second[:], in1=base_of[u][:, a, :], op=ADD
                )
                j = (u % UNITS_PER_CHUNK) * UNIT_BLOCKS + a
                nc.sync.dma_start(out=out_v[u // UNITS_PER_CHUNK][:, j, :], in_=result[:, a, :])

        for k in range(UNITS + 2):
            if k < UNITS:
                transpose_and_quantise(k)
                if k == 0:
                    broadcast_bias()
                add_bias_to_residual(k)
            if 1 <= k <= UNITS:
                first_product(k - 1)
            if k >= 2:
                second_product(k - 2)
